import numpy as np
import ml_dtypes


def mxq(x, axis, fmt="e4m3"):
    dtype, down = {"e4m3": (ml_dtypes.float8_e4m3fn, 7), "e5m2": (ml_dtypes.float8_e5m2, 14)}[fmt]
    v = np.moveaxis(np.asarray(x, np.float32).astype(ml_dtypes.bfloat16).astype(np.float64), axis, -1)
    blocks = v.reshape(v.shape[:-1] + (-1, 32))
    amax = np.abs(blocks).max(-1, keepdims=True)
    byte = np.maximum(np.where(amax > 0, np.frexp(amax)[1] - 1 + 127, 0) - down, 1)
    scale = np.exp2(byte - 127.0)
    codes = (blocks / scale).astype(np.float32).astype(dtype).astype(np.float64)
    return np.moveaxis((codes * scale).reshape(v.shape), -1, axis)


WIDE = False


def mx_kscale(k):
    if not WIDE:
        return np.ones(k)
    levels = np.array([10, -10, 5, -5, 0])
    if k % 512:
        return np.exp2(np.random.permutation(np.resize(levels, k // 32))).repeat(32)
    a = np.empty((k // 512, 16))
    for p in range(k // 512):
        a[p, :8] = np.random.permutation(np.resize(levels, 8))
        for g in range(8):
            far = levels[np.abs(levels - a[p, g]) >= 10]
            a[p, g + 8] = far[np.random.randint(len(far))]
    return np.exp2(a.ravel()).repeat(32)


BF16 = ml_dtypes.bfloat16


def bf(x):
    return np.asarray(x, np.float32).astype(BF16)


def f64(x):
    return np.asarray(x).astype(np.float64)


B, L, H, G, DEPTH = 64, 64, 512, 256, 3
EPS = 1e-5


def layernorm(v, g, b):
    mu = v.mean(-1, keepdims=True)
    var = np.square(v - mu).mean(-1, keepdims=True)
    return (v - mu) / np.sqrt(var + EPS) * g + b


def setup_inputs():
    s, t = mx_kscale(H), mx_kscale(H)
    return {"x_nodes": bf(np.random.standard_normal((B, L, H)) * s),
            "w1": bf(np.random.standard_normal((H, H)) / np.sqrt(H) / s[:, None]),
            "b1": bf(np.random.standard_normal(H) * 0.3),
            "gamma": bf((1.0 + 0.1 * np.random.standard_normal(H)) * t),
            "beta": bf(0.2 * np.random.standard_normal(H) * t),
            "w2": bf(np.random.standard_normal((H, G)) / np.sqrt(H) / t[:, None]),
            "b2": bf(np.random.standard_normal(G) * 0.3)}


def reference(x_nodes, w1, b1, gamma, beta, w2, b2):
    h = (mxq(f64(x_nodes), 2, "e4m3") @ mxq(f64(w1), 0, "e4m3")) + f64(b1)
    r = np.maximum(layernorm(h, f64(gamma), f64(beta)), 0.0)
    x1 = (mxq(r, 2, "e4m3") @ mxq(f64(w2), 0, "e4m3")) + f64(b2)
    x2 = np.broadcast_to(x1.max(axis=1, keepdims=True), x1.shape)
    return np.concatenate([x1, x2], axis=2)

@@ -1,0 +1,409 @@
+from contextlib import ExitStack
+
+import concourse.mybir as mybir
+from concourse.masks import make_identity
+
+F32 = mybir.dt.float32
+BF16 = mybir.dt.bfloat16
+U32 = mybir.dt.uint32
+U8 = mybir.dt.uint8
+FP8X4 = mybir.dt.float8_e4m3fn_x4
+ALU = mybir.AluOpType
+ACT = mybir.ActivationFunctionType
+AXIS = mybir.AxisListType
+
+P = 128
+PACK = 4
+TOKENS = 64 * 64
+NODES = 64
+H = 512
+G = 256
+EPS = 1e-5
+
+TILES = 2
+UNIT = TILES * P
+N_UNITS = TOKENS // UNIT
+UNITS_PER_GROUP = 2
+GROUP = UNITS_PER_GROUP * UNIT
+LINES_PER_UNIT = UNIT // NODES
+LINES_PER_GROUP = GROUP // NODES
+COPIES = P // LINES_PER_GROUP
+ROWS_PER_COPY = NODES // COPIES
+HALVES = G // P
+RUN = 4
+
+S_TRANSPOSE_X = 0
+S_COPY_X = 1
+S_FIRST = 2
+S_NORM = 3
+S_FEATURES = 4
+S_QUANTISE_R = 5
+S_SECOND = 6
+S_OUTPUTS = 7
+S_POOL = 8
+
+FLOPS = 2 * TOKENS * H * H + 2 * TOKENS * H * G
+
+
+def tile_sub_graph_pa_kernel(tc, x_nodes, w1, b1, gamma, beta, w2, b2, out):
+    nc = tc.nc
+    x_flat = x_nodes.flatten_outer_dims()
+    out_flat = out.flatten_outer_dims()
+
+    with ExitStack() as ctx:
+        ctx.enter_context(tc.manual_schedule())
+        const = ctx.enter_context(tc.tile_pool(name="const", bufs=1))
+        per_unit = ctx.enter_context(tc.tile_pool(name="per_unit", bufs=4))
+        per_tile = ctx.enter_context(tc.tile_pool(name="per_tile", bufs=4 * TILES))
+        psum_x = ctx.enter_context(tc.psum_pool(name="psum_x", bufs=1))
+        psum_h = ctx.enter_context(tc.psum_pool(name="psum_h", bufs=2))
+        psum_z = ctx.enter_context(tc.psum_pool(name="psum_z", bufs=2))
+        psum_a = ctx.enter_context(tc.psum_pool(name="psum_a", bufs=1))
+        psum_b = ctx.enter_context(tc.psum_pool(name="psum_b", bufs=1))
+        psum_s = ctx.enter_context(tc.psum_pool(name="psum_s", bufs=1))
+
+        w1_raw = const.tile([P, PACK, H], BF16)
+        nc.sync.dma_start(out=w1_raw[:], in_=w1.rearrange("(p j) c -> p j c", j=PACK))
+        x_tiles = []
+        for unit in range(N_UNITS):
+            x_sb = const.tile([P, TILES, H], BF16, name="x_sb%d" % unit)
+            x_tiles.append(x_sb)
+
+        def load_x(unit):
+            nc.sync.dma_start(
+                out=x_tiles[unit][:],
+                in_=x_flat[unit * UNIT : (unit + 1) * UNIT, :].rearrange("(j p) k -> p j k", p=P),
+            )
+
+        load_x(0)
+        w2_raw = const.tile([P, PACK, G], BF16)
+        nc.sync.dma_start(out=w2_raw[:], in_=w2.rearrange("(p j) n -> p j n", j=PACK))
+        for unit in range(1, N_UNITS):
+            load_x(unit)
+
+        ident = const.tile([P, P], F32)
+        make_identity(nc, ident[:])
+        eps = const.tile([P, 1], F32)
+        nc.vector.memset(eps[:], EPS)
+        warm = const.tile([P, 1], F32)
+        nc.scalar.activation(out=warm[:], in_=eps[:], func=ACT.Abs_reciprocal_sqrt)
+
+        bias_in = const.tile([P, H + G], BF16)
+        nc.vector.memset(bias_in[:], 0.0)
+        nc.scalar.dma_start(out=bias_in[0:1, 0:H], in_=b1.rearrange("(o k) -> o k", o=1))
+        nc.scalar.dma_start(out=bias_in[0:1, H : H + G], in_=b2.rearrange("(o k) -> o k", o=1))
+        ones = const.tile([P, P], BF16)
+        nc.vector.memset(ones[:], 1.0)
+        affine_bf = const.tile([P, 2, 16], BF16)
+        nc.scalar.dma_start(out=affine_bf[:, 0, 0:PACK], in_=gamma.rearrange("(p t) -> p t", t=PACK))
+        nc.scalar.dma_start(out=affine_bf[:, 1, 0:PACK], in_=beta.rearrange("(p t) -> p t", t=PACK))
+        affine = const.tile([P, 2, PACK], F32)
+        rows_bf = const.tile([P, P], BF16)
+        nc.vector.memset(rows_bf[:], 0.0)
+        nc.scalar.dma_start(out=rows_bf[0:2, :], in_=b2.rearrange("(t p) -> t p", p=P))
+
+        rows_f32 = const.tile([P, P], F32)
+        nc.vector.tensor_copy(out=rows_f32[:], in_=rows_bf[:])
+        nc.vector.tensor_copy(out=affine[:], in_=affine_bf[:, :, 0:PACK])
+        cols = const.tile([P, 16], F32)
+        b1_rows = const.tile([P, H], F32)
+        b2_rows = const.tile([P, G], F32)
+
+        def spread_constants():
+            cols_ps = psum_s.tile([P, P], F32, tag="small")
+            nc.tensor.transpose(cols_ps[:], rows_f32[:], ident[:])
+            nc.scalar.copy(out=cols[:], in_=cols_ps[:, 0:16])
+            b1_ps = psum_h.tile([P, H], F32, tag="h_ps")
+            nc.tensor.matmul(out=b1_ps[:], lhsT=ones[:], rhs=bias_in[:, 0:H], start=True, stop=True)
+            nc.scalar.copy(out=b1_rows[:].rearrange("p (t m) -> p t m", t=PACK), in_=b1_ps[:].rearrange("p (m t) -> p t m", t=PACK))
+            b2_ps = psum_h.tile([P, H], F32, tag="h_ps")
+            nc.tensor.matmul(out=b2_ps[:, 0:G], lhsT=ones[:], rhs=bias_in[:, H : H + G], start=True, stop=True)
+            nc.scalar.copy(out=b2_rows[:], in_=b2_ps[:, 0:G])
+
+        def gamma_col(t):
+            return affine[:, 0, t : t + 1]
+
+        def beta_col(t):
+            return affine[:, 1, t : t + 1]
+
+        def b2_col(c):
+            return cols[:, c : c + 1]
+
+        def quantise_weight(raw, width, label, permute):
+            grouped = const.tile([P, width, PACK], BF16, align_bytes=64, name=label + "_grouped")
+            if permute:
+                nc.vector.tensor_copy(
+                    out=grouped[:].rearrange("p (t m) j -> p t m j", t=PACK),
+                    in_=raw[:].rearrange("p j (m t) -> p t m j", t=PACK),
+                )
+            else:
+                nc.vector.tensor_copy(
+                    out=grouped[:].rearrange("p (c i) t -> p c t i", i=RUN),
+                    in_=raw[:].rearrange("p t (c i) -> p c t i", i=RUN),
+                )
+            codes = const.tile([P, width], U32, align_bytes=64, name=label + "_codes")
+            scales = const.tile([P, width], U8, align_bytes=64, name=label + "_scales")
+            nc.vector.quantize_mx(
+                out=codes[:].bitcast(FP8X4),
+                scales=scales[:],
+                in_=grouped[:].rearrange("p c t -> p (c t)"),
+            )
+            return codes, scales
+
+        w1_codes, w1_scales = quantise_weight(w1_raw, H, "w1", True)
+        w2_q = {}
+
+        live = {}
+        units = range(N_UNITS)
+
+        def transpose_x(unit):
+            if unit not in units:
+                return
+            xt_ps = psum_x.tile([P, TILES, 2, P], F32)
+            for j in range(TILES):
+                words = x_tiles[unit][:, j, :].bitcast(F32)
+                for u in range(2):
+                    nc.tensor.transpose(xt_ps[:, j, u, :], words[:, u::2], ident[:])
+            live["xt_ps", unit] = xt_ps
+
+        def copy_x(unit):
+            if unit not in units:
+                return
+            x_words = per_unit.tile([P, TILES, P, 2], F32, align_bytes=64)
+            nc.scalar.copy(out=x_words[:], in_=live.pop(("xt_ps", unit))[:].rearrange("p j u r -> p j r u"))
+            live["x_words", unit] = x_words
+
+        def first_matmul(unit):
+            if unit not in units:
+                return
+            x_words = live.pop(("x_words", unit))
+            x_codes = per_unit.tile([P, UNIT], U32, align_bytes=64)
+            x_scales = per_unit.tile([P, UNIT], U8, align_bytes=64)
+            nc.vector.quantize_mx(
+                out=x_codes[:].bitcast(FP8X4),
+                scales=x_scales[:],
+                in_=x_words[:].rearrange("p j r u -> p (j r u)").bitcast(BF16),
+            )
+            for j in range(TILES):
+                tokens = slice(j * P, (j + 1) * P)
+                h_ps = psum_h.tile([P, H], F32, tag="h_ps")
+                nc.tensor.matmul_mx(
+                    out=h_ps[:],
+                    lhsT=x_codes[:, tokens].bitcast(FP8X4),
+                    lhsT_scale=x_scales[:, tokens],
+                    rhs=w1_codes[:].bitcast(FP8X4),
+                    rhs_scale=w1_scales[:],
+                    start=True,
+                    stop=True,
+                )
+                live["h_ps", unit, j] = h_ps
+
+        def bias_and_squares(unit):
+            if unit not in units:
+                return
+            h_sum = per_unit.tile([P, TILES], F32)
+            sq_sum = per_unit.tile([P, TILES], F32)
+            h_tiles = []
+            for j in range(TILES):
+                h = per_tile.tile([P, H], F32)
+                nc.vector.scalar_tensor_tensor(
+                    out=h[:],
+                    in0=live.pop(("h_ps", unit, j))[:],
+                    scalar=1.0,
+                    in1=b1_rows[:],
+                    op0=ALU.mult,
+                    op1=ALU.add,
+                    accum_out=h_sum[:, j : j + 1],
+                )
+                h_tiles.append(h)
+            for j in range(TILES):
+                squares = per_tile.tile([P, H], BF16)
+                nc.scalar.activation(
+                    out=squares[:],
+                    in_=h_tiles[j][:],
+                    func=ACT.Square,
+                    bias=h_sum[:, j : j + 1],
+                    scale=-1.0 * H,
+                    accum_out=sq_sum[:, j : j + 1],
+                )
+            live["h", unit] = h_tiles
+            live["h_sum", unit] = h_sum
+            live["sq_sum", unit] = sq_sum
+
+        def normalise(unit):
+            if unit not in units:
+                return
+            h_tiles = live.pop(("h", unit))
+            h_sum = live.pop(("h_sum", unit))
+            sq_sum = live.pop(("sq_sum", unit))
+            neg_mean = per_unit.tile([P, TILES], F32)
+            nc.scalar.mul(out=neg_mean[:], in_=h_sum[:], mul=-1.0 / H)
+            rstd = per_unit.tile([P, TILES], F32)
+            nc.scalar.activation(
+                out=rstd[:], in_=sq_sum[:], func=ACT.Abs_reciprocal_sqrt, bias=eps[:], scale=1.0 / (H * H * H)
+            )
+            for j in range(TILES):
+                z = per_tile.tile([P, H], F32)
+                nc.gpsimd.tensor_scalar(
+                    out=z[:],
+                    in0=h_tiles[j][:],
+                    scalar1=neg_mean[:, j : j + 1],
+                    scalar2=rstd[:, j : j + 1],
+                    op0=ALU.add,
+                    op1=ALU.mult,
+                )
+                live["z", unit, j] = z
+
+        def to_features(unit):
+            if unit not in units:
+                return
+            z_tiles = [live.pop(("z", unit, j)) for j in range(TILES)]
+            r_planes = per_unit.tile([P, PACK, UNIT], BF16)
+            z_banks = []
+            for pair in range(PACK // 2):
+                z_ps = psum_z.tile([P, 2, UNIT], F32)
+                z_banks.append(z_ps)
+            for j in range(TILES):
+                for t in range(PACK):
+                    nc.tensor.transpose(
+                        z_banks[t // 2][:, t % 2, j * P : (j + 1) * P], z_tiles[j][:, t * P : (t + 1) * P], ident[:]
+                    )
+            for t in range(PACK):
+                nc.scalar.activation(
+                    out=r_planes[:, t, :],
+                    in_=z_banks[t // 2][:, t % 2, :],
+                    func=ACT.Relu,
+                    bias=beta_col(t),
+                    scale=gamma_col(t),
+                )
+            live["r_planes", unit] = r_planes
+
+        def regroup_r(unit):
+            if unit not in units:
+                return
+            r_planes = live.pop(("r_planes", unit))
+            r_grouped = per_unit.tile([P, UNIT, PACK], BF16, align_bytes=64)
+            nc.vector.tensor_copy(
+                out=r_grouped[:].rearrange("p (c i) t -> p c t i", i=RUN),
+                in_=r_planes[:].rearrange("p t (c i) -> p c t i", i=RUN),
+            )
+            live["r_grouped", unit] = r_grouped
+
+        def quantise_r(unit):
+            if unit not in units:
+                return
+            r_grouped = live.pop(("r_grouped", unit))
+            r_codes = per_unit.tile([P, UNIT], U32, align_bytes=64)
+            r_scales = per_unit.tile([P, UNIT], U8, align_bytes=64)
+            nc.vector.quantize_mx(
+                out=r_codes[:].bitcast(FP8X4),
+                scales=r_scales[:],
+                in_=r_grouped[:].rearrange("p r t -> p (r t)"),
+            )
+            live["r_codes", unit] = r_codes
+            live["r_scales", unit] = r_scales
+
+        def second_matmuls(unit):
+            if unit not in units:
+                return
+            r_codes = live.pop(("r_codes", unit))
+            r_scales = live.pop(("r_scales", unit))
+            w2_codes, w2_scales = w2_q["codes"], w2_q["scales"]
+            x1_ps = psum_a.tile([P, TILES, G], F32)
+            for j in range(TILES):
+                tokens = slice(j * P, (j + 1) * P)
+                nc.tensor.matmul_mx(
+                    out=x1_ps[:, j, :],
+                    lhsT=r_codes[:, tokens].bitcast(FP8X4),
+                    lhsT_scale=r_scales[:, tokens],
+                    rhs=w2_codes[:].bitcast(FP8X4),
+                    rhs_scale=w2_scales[:],
+                    start=True,
+                    stop=True,
+                )
+            x1t_ps = psum_b.tile([P, HALVES, UNIT], F32)
+            for c in range(HALVES):
+                channels = slice(c * P, (c + 1) * P)
+                nc.tensor.matmul_mx(
+                    out=x1t_ps[:, c, :],
+                    lhsT=w2_codes[:, channels].bitcast(FP8X4),
+                    lhsT_scale=w2_scales[:, channels],
+                    rhs=r_codes[:].bitcast(FP8X4),
+                    rhs_scale=r_scales[:],
+                    start=True,
+                    stop=True,
+                )
+            live["x1_ps", unit] = x1_ps
+            live["x1t_ps", unit] = x1t_ps
+
+        def outputs(unit):
+            if unit not in units:
+                return
+            g, part = divmod(unit, UNITS_PER_GROUP)
+            x1 = per_unit.tile([P, TILES, G], F32)
+            nc.vector.tensor_tensor(
+                out=x1[:],
+                in0=live.pop(("x1_ps", unit))[:],
+                in1=b2_rows[:].unsqueeze(1).to_broadcast([P, TILES, G]),
+                op=ALU.add,
+            )
+            nc.sync.dma_start(
+                out=out_flat[unit * UNIT : (unit + 1) * UNIT, 0:G].rearrange("(j p) c -> p j c", p=P),
+                in_=x1[:],
+            )
+            if part == 0:
+                pooled_new = per_unit.tile([P, HALVES, LINES_PER_GROUP], F32)
+                live["pooled", g] = pooled_new
+            pooled = live["pooled", g]
+            nc.vector.tensor_reduce(
+                out=pooled[:, :, part * LINES_PER_UNIT : (part + 1) * LINES_PER_UNIT],
+                in_=live.pop(("x1t_ps", unit))[:].rearrange("p c (b l) -> p c b l", l=NODES),
+                axis=AXIS.X,
+                op=ALU.max,
+            )
+
+        def pool(unit):
+            g, part = divmod(unit, UNITS_PER_GROUP)
+            if unit not in units or part < UNITS_PER_GROUP - 1:
+                return
+            pooled = live.pop(("pooled", g))
+            spread = per_unit.tile([P, HALVES, LINES_PER_GROUP, COPIES], F32)
+            x2_ps = psum_s.tile([P, G], F32, tag="small")
+            for c in range(HALVES):
+                nc.vector.tensor_scalar(
+                    out=spread[:, c, :, :],
+                    in0=pooled[:, c, :].unsqueeze(2).to_broadcast([P, LINES_PER_GROUP, COPIES]),
+                    scalar1=b2_col(c),
+                    scalar2=None,
+                    op0=ALU.add,
+                )
+                nc.tensor.transpose(
+                    x2_ps[:, c * P : (c + 1) * P],
+                    spread[:, c, :, :].rearrange("p b d -> p (b d)"),
+                    ident[:],
+                )
+            x2 = per_unit.tile([P, G], F32)
+            nc.scalar.copy(out=x2[:], in_=x2_ps[:])
+            nc.sync.dma_start(
+                out=out_flat[g * GROUP : (g + 1) * GROUP, G : 2 * G].rearrange(
+                    "(q i) c -> q i c", i=ROWS_PER_COPY
+                ),
+                in_=x2[:].unsqueeze(1).to_broadcast([P, ROWS_PER_COPY, G]),
+            )
+
+        for k in range(N_UNITS + S_POOL):
+            outputs(k - S_OUTPUTS)
+            second_matmuls(k - S_SECOND)
+            bias_and_squares(k - S_NORM)
+            copy_x(k - S_COPY_X)
+            normalise(k - S_NORM)
+            to_features(k - S_FEATURES)
+            regroup_r(k - S_QUANTISE_R)
+            first_matmul(k - S_FIRST)
+            pool(k - S_POOL)
+            quantise_r(k - S_QUANTISE_R)
+            transpose_x(k - S_TRANSPOSE_X)
+            if k == S_COPY_X:
+                spread_constants()
+            if k == S_FEATURES:
+                w2_q["codes"], w2_q["scales"] = quantise_weight(w2_raw, G, "w2", False)

@@ -76,6 +76,15 @@ def tile_sub_graph_pa_kernel(tc, x_nodes, w1, b1, gamma, beta, w2, b2, out):
             )
 
         load_x(0)
+
+        bias_in = const.tile([P, H + G], BF16)
+        nc.vector.memset(bias_in[:], 0.0)
+        nc.scalar.dma_start(out=bias_in[0:1, 0:H], in_=b1.rearrange("(o k) -> o k", o=1))
+        nc.scalar.dma_start(out=bias_in[0:1, H : H + G], in_=b2.rearrange("(o k) -> o k", o=1))
+        affine_bf = const.tile([P, 2, 16], BF16)
+        nc.scalar.dma_start(out=affine_bf[:, 0, 0:PACK], in_=gamma.rearrange("(p t) -> p t", t=PACK))
+        nc.scalar.dma_start(out=affine_bf[:, 1, 0:PACK], in_=beta.rearrange("(p t) -> p t", t=PACK))
+
         w2_raw = const.tile([P, PACK, G], BF16)
         nc.sync.dma_start(out=w2_raw[:], in_=w2.rearrange("(p j) n -> p j n", j=PACK))
         for unit in range(1, N_UNITS):
@@ -83,42 +92,36 @@ def tile_sub_graph_pa_kernel(tc, x_nodes, w1, b1, gamma, beta, w2, b2, out):
 
         ident = const.tile([P, P], F32)
         make_identity(nc, ident[:])
+        ones = const.tile([P, P], BF16)
+        nc.vector.memset(ones[:], 1.0)
         eps = const.tile([P, 1], F32)
         nc.vector.memset(eps[:], EPS)
         warm = const.tile([P, 1], F32)
         nc.scalar.activation(out=warm[:], in_=eps[:], func=ACT.Abs_reciprocal_sqrt)
 
-        bias_in = const.tile([P, H + G], BF16)
-        nc.vector.memset(bias_in[:], 0.0)
-        nc.scalar.dma_start(out=bias_in[0:1, 0:H], in_=b1.rearrange("(o k) -> o k", o=1))
-        nc.scalar.dma_start(out=bias_in[0:1, H : H + G], in_=b2.rearrange("(o k) -> o k", o=1))
-        ones = const.tile([P, P], BF16)
-        nc.vector.memset(ones[:], 1.0)
-        affine_bf = const.tile([P, 2, 16], BF16)
-        nc.scalar.dma_start(out=affine_bf[:, 0, 0:PACK], in_=gamma.rearrange("(p t) -> p t", t=PACK))
-        nc.scalar.dma_start(out=affine_bf[:, 1, 0:PACK], in_=beta.rearrange("(p t) -> p t", t=PACK))
         affine = const.tile([P, 2, PACK], F32)
-        rows_bf = const.tile([P, P], BF16)
-        nc.vector.memset(rows_bf[:], 0.0)
-        nc.scalar.dma_start(out=rows_bf[0:2, :], in_=b2.rearrange("(t p) -> t p", p=P))
-
-        rows_f32 = const.tile([P, P], F32)
-        nc.vector.tensor_copy(out=rows_f32[:], in_=rows_bf[:])
-        nc.vector.tensor_copy(out=affine[:], in_=affine_bf[:, :, 0:PACK])
-        cols = const.tile([P, 16], F32)
+        b2_cols = const.tile([P, HALVES], F32)
         b1_rows = const.tile([P, H], F32)
         b2_rows = const.tile([P, G], F32)
 
         def spread_constants():
-            cols_ps = psum_s.tile([P, P], F32, tag="small")
-            nc.tensor.transpose(cols_ps[:], rows_f32[:], ident[:])
-            nc.scalar.copy(out=cols[:], in_=cols_ps[:, 0:16])
             b1_ps = psum_h.tile([P, H], F32, tag="h_ps")
             nc.tensor.matmul(out=b1_ps[:], lhsT=ones[:], rhs=bias_in[:, 0:H], start=True, stop=True)
-            nc.scalar.copy(out=b1_rows[:].rearrange("p (t m) -> p t m", t=PACK), in_=b1_ps[:].rearrange("p (m t) -> p t m", t=PACK))
+            nc.scalar.copy(
+                out=b1_rows[:].rearrange("p (t m) -> p t m", t=PACK),
+                in_=b1_ps[:].rearrange("p (m t) -> p t m", t=PACK),
+            )
             b2_ps = psum_h.tile([P, H], F32, tag="h_ps")
             nc.tensor.matmul(out=b2_ps[:, 0:G], lhsT=ones[:], rhs=bias_in[:, H : H + G], start=True, stop=True)
             nc.scalar.copy(out=b2_rows[:], in_=b2_ps[:, 0:G])
+            cols_ps = psum_s.tile([P, G], F32, tag="small")
+            for c in range(HALVES):
+                channels = slice(H + c * P, H + (c + 1) * P)
+                nc.tensor.matmul(
+                    out=cols_ps[:, c : c + 1], lhsT=bias_in[:, channels], rhs=ones[:, 0:1], start=True, stop=True
+                )
+            nc.scalar.copy(out=b2_cols[:], in_=cols_ps[:, 0:HALVES])
+            nc.vector.tensor_copy(out=affine[:], in_=affine_bf[:, :, 0:PACK])
 
         def gamma_col(t):
             return affine[:, 0, t : t + 1]
@@ -127,7 +130,7 @@ def tile_sub_graph_pa_kernel(tc, x_nodes, w1, b1, gamma, beta, w2, b2, out):
             return affine[:, 1, t : t + 1]
 
         def b2_col(c):
-            return cols[:, c : c + 1]
+            return b2_cols[:, c : c + 1]
 
         def quantise_weight(raw, width, label, permute):
             grouped = const.tile([P, width, PACK], BF16, align_bytes=64, name=label + "_grouped")

@@ -78,7 +78,7 @@ def tile_sub_graph_pa_kernel(tc, x_nodes, w1, b1, gamma, beta, w2, b2, out):
         load_x(0)
 
         bias_in = const.tile([P, H + G], BF16)
-        nc.vector.memset(bias_in[:], 0.0)
+        nc.gpsimd.memset(bias_in[:].bitcast(F32), 0.0)
         nc.scalar.dma_start(out=bias_in[0:1, 0:H], in_=b1.rearrange("(o k) -> o k", o=1))
         nc.scalar.dma_start(out=bias_in[0:1, H : H + G], in_=b2.rearrange("(o k) -> o k", o=1))
         affine_bf = const.tile([P, 2, 16], BF16)
@@ -105,13 +105,13 @@ def tile_sub_graph_pa_kernel(tc, x_nodes, w1, b1, gamma, beta, w2, b2, out):
         b2_rows = const.tile([P, G], F32)
 
         def spread_constants():
-            b1_ps = psum_h.tile([P, H], F32, tag="h_ps")
+            b1_ps = psum_a.tile([P, H], F32, tag="x1_ps")
             nc.tensor.matmul(out=b1_ps[:], lhsT=ones[:], rhs=bias_in[:, 0:H], start=True, stop=True)
             nc.scalar.copy(
                 out=b1_rows[:].rearrange("p (t m) -> p t m", t=PACK),
                 in_=b1_ps[:].rearrange("p (m t) -> p t m", t=PACK),
             )
-            b2_ps = psum_h.tile([P, H], F32, tag="h_ps")
+            b2_ps = psum_b.tile([P, H], F32, tag="x1t_ps")
             nc.tensor.matmul(out=b2_ps[:, 0:G], lhsT=ones[:], rhs=bias_in[:, H : H + G], start=True, stop=True)
             nc.scalar.copy(out=b2_rows[:], in_=b2_ps[:, 0:G])
             cols_ps = psum_s.tile([P, G], F32, tag="small")
@@ -312,7 +312,7 @@ def tile_sub_graph_pa_kernel(tc, x_nodes, w1, b1, gamma, beta, w2, b2, out):
             r_codes = live.pop(("r_codes", unit))
             r_scales = live.pop(("r_scales", unit))
             w2_codes, w2_scales = w2_q["codes"], w2_q["scales"]
-            x1_ps = psum_a.tile([P, TILES, G], F32)
+            x1_ps = psum_a.tile([P, TILES, G], F32, tag="x1_ps")
             for j in range(TILES):
                 tokens = slice(j * P, (j + 1) * P)
                 nc.tensor.matmul_mx(
@@ -324,7 +324,7 @@ def tile_sub_graph_pa_kernel(tc, x_nodes, w1, b1, gamma, beta, w2, b2, out):
                     start=True,
                     stop=True,
                 )
-            x1t_ps = psum_b.tile([P, HALVES, UNIT], F32)
+            x1t_ps = psum_b.tile([P, HALVES, UNIT], F32, tag="x1t_ps")
             for c in range(HALVES):
                 channels = slice(c * P, (c + 1) * P)
                 nc.tensor.matmul_mx(
@@ -365,21 +365,28 @@ def tile_sub_graph_pa_kernel(tc, x_nodes, w1, b1, gamma, beta, w2, b2, out):
                 op=ALU.max,
             )
 
-        def pool(unit):
+        def spread_maxima(unit):
             g, part = divmod(unit, UNITS_PER_GROUP)
             if unit not in units or part < UNITS_PER_GROUP - 1:
                 return
             pooled = live.pop(("pooled", g))
             spread = per_unit.tile([P, HALVES, LINES_PER_GROUP, COPIES], F32)
+            for c in range(HALVES):
+                nc.scalar.activation(
+                    out=spread[:, c, :, :],
+                    in_=pooled[:, c, :].unsqueeze(2).to_broadcast([P, LINES_PER_GROUP, COPIES]),
+                    func=ACT.Identity,
+                    bias=b2_col(c),
+                )
+            live["spread", g] = spread
+
+        def pool(unit):
+            g, part = divmod(unit, UNITS_PER_GROUP)
+            if unit not in units or part < UNITS_PER_GROUP - 1:
+                return
+            spread = live.pop(("spread", g))
             x2_ps = psum_s.tile([P, G], F32, tag="small")
             for c in range(HALVES):
-                nc.vector.tensor_scalar(
-                    out=spread[:, c, :, :],
-                    in0=pooled[:, c, :].unsqueeze(2).to_broadcast([P, LINES_PER_GROUP, COPIES]),
-                    scalar1=b2_col(c),
-                    scalar2=None,
-                    op0=ALU.add,
-                )
                 nc.tensor.transpose(
                     x2_ps[:, c * P : (c + 1) * P],
                     spread[:, c, :, :].rearrange("p b d -> p (b d)"),
@@ -395,6 +402,7 @@ def tile_sub_graph_pa_kernel(tc, x_nodes, w1, b1, gamma, beta, w2, b2, out):
             )
 
         for k in range(N_UNITS + S_POOL):
+            spread_maxima(k - S_POOL)
             outputs(k - S_OUTPUTS)
             second_matmuls(k - S_SECOND)
             bias_and_squares(k - S_NORM)

@@ -20,27 +20,27 @@ H = 512
 G = 256
 EPS = 1e-5
 
-TILES = 2
-UNIT = TILES * P
-N_UNITS = TOKENS // UNIT
-UNITS_PER_GROUP = 2
-GROUP = UNITS_PER_GROUP * UNIT
-LINES_PER_UNIT = UNIT // NODES
-LINES_PER_GROUP = GROUP // NODES
-COPIES = P // LINES_PER_GROUP
-ROWS_PER_COPY = NODES // COPIES
+TILES = TOKENS // P
+LINES_PER_TILE = P // NODES
+UNIT_TILES = (1, 1) + 14 * (2,) + (1, 1)
+GROUP_TILES = 8 * (4,)
 HALVES = G // P
 RUN = 4
 
 S_TRANSPOSE_X = 0
 S_COPY_X = 1
-S_FIRST = 2
-S_NORM = 3
-S_FEATURES = 4
-S_QUANTISE_R = 5
-S_SECOND = 6
-S_OUTPUTS = 7
-S_POOL = 8
+S_QUANTISE_X = 2
+S_FIRST = 3
+S_NORM = 4
+S_FEATURES = 6
+S_QUANTISE_R = 7
+S_SECOND = 8
+S_OUTPUTS = 9
+S_POOL = 10
+
+N_UNITS = len(UNIT_TILES)
+UNIT_START = [sum(UNIT_TILES[:n]) for n in range(N_UNITS)]
+GROUP_START = [sum(GROUP_TILES[:n]) for n in range(len(GROUP_TILES))]
 
 FLOPS = 2 * TOKENS * H * H + 2 * TOKENS * H * G
 
@@ -54,25 +54,28 @@ def tile_sub_graph_pa_kernel(tc, x_nodes, w1, b1, gamma, beta, w2, b2, out):
         ctx.enter_context(tc.manual_schedule())
         const = ctx.enter_context(tc.tile_pool(name="const", bufs=1))
         per_unit = ctx.enter_context(tc.tile_pool(name="per_unit", bufs=4))
-        per_tile = ctx.enter_context(tc.tile_pool(name="per_tile", bufs=4 * TILES))
-        psum_x = ctx.enter_context(tc.psum_pool(name="psum_x", bufs=1))
+        per_tile = ctx.enter_context(tc.tile_pool(name="per_tile", bufs=8))
+        psum_x = ctx.enter_context(tc.psum_pool(name="psum_x", bufs=2))
         psum_h = ctx.enter_context(tc.psum_pool(name="psum_h", bufs=2))
         psum_z = ctx.enter_context(tc.psum_pool(name="psum_z", bufs=2))
         psum_a = ctx.enter_context(tc.psum_pool(name="psum_a", bufs=1))
         psum_b = ctx.enter_context(tc.psum_pool(name="psum_b", bufs=1))
-        psum_s = ctx.enter_context(tc.psum_pool(name="psum_s", bufs=1))
 
         w1_raw = const.tile([P, PACK, H], BF16)
         nc.sync.dma_start(out=w1_raw[:], in_=w1.rearrange("(p j) c -> p j c", j=PACK))
         x_tiles = []
         for unit in range(N_UNITS):
-            x_sb = const.tile([P, TILES, H], BF16, name="x_sb%d" % unit)
+            x_sb = const.tile([P, UNIT_TILES[unit], H], BF16, name="x_sb%d" % unit)
             x_tiles.append(x_sb)
+
+        def rows_of(unit):
+            start = UNIT_START[unit] * P
+            return slice(start, start + UNIT_TILES[unit] * P)
 
         def load_x(unit):
             nc.sync.dma_start(
                 out=x_tiles[unit][:],
-                in_=x_flat[unit * UNIT : (unit + 1) * UNIT, :].rearrange("(j p) k -> p j k", p=P),
+                in_=x_flat[rows_of(unit), :].rearrange("(j p) k -> p j k", p=P),
             )
 
         load_x(0)
@@ -85,9 +88,10 @@ def tile_sub_graph_pa_kernel(tc, x_nodes, w1, b1, gamma, beta, w2, b2, out):
         nc.scalar.dma_start(out=affine_bf[:, 0, 0:PACK], in_=gamma.rearrange("(p t) -> p t", t=PACK))
         nc.scalar.dma_start(out=affine_bf[:, 1, 0:PACK], in_=beta.rearrange("(p t) -> p t", t=PACK))
 
+        load_x(1)
         w2_raw = const.tile([P, PACK, G], BF16)
         nc.sync.dma_start(out=w2_raw[:], in_=w2.rearrange("(p j) n -> p j n", j=PACK))
-        for unit in range(1, N_UNITS):
+        for unit in range(2, N_UNITS):
             load_x(unit)
 
         ident = const.tile([P, P], F32)
@@ -104,24 +108,25 @@ def tile_sub_graph_pa_kernel(tc, x_nodes, w1, b1, gamma, beta, w2, b2, out):
         b1_rows = const.tile([P, H], F32)
         b2_rows = const.tile([P, G], F32)
 
-        def spread_constants():
+        def spread_b1():
             b1_ps = psum_a.tile([P, H], F32, tag="x1_ps")
             nc.tensor.matmul(out=b1_ps[:], lhsT=ones[:], rhs=bias_in[:, 0:H], start=True, stop=True)
             nc.scalar.copy(
                 out=b1_rows[:].rearrange("p (t m) -> p t m", t=PACK),
                 in_=b1_ps[:].rearrange("p (m t) -> p t m", t=PACK),
             )
+
+        def spread_b2():
             b2_ps = psum_b.tile([P, H], F32, tag="x1t_ps")
             nc.tensor.matmul(out=b2_ps[:, 0:G], lhsT=ones[:], rhs=bias_in[:, H : H + G], start=True, stop=True)
             nc.scalar.copy(out=b2_rows[:], in_=b2_ps[:, 0:G])
-            cols_ps = psum_s.tile([P, G], F32, tag="small")
+            cols_ps = psum_a.tile([P, H], F32, tag="x1_ps")
             for c in range(HALVES):
                 channels = slice(H + c * P, H + (c + 1) * P)
                 nc.tensor.matmul(
                     out=cols_ps[:, c : c + 1], lhsT=bias_in[:, channels], rhs=ones[:, 0:1], start=True, stop=True
                 )
             nc.scalar.copy(out=b2_cols[:], in_=cols_ps[:, 0:HALVES])
-            nc.vector.tensor_copy(out=affine[:], in_=affine_bf[:, :, 0:PACK])
 
         def gamma_col(t):
             return affine[:, 0, t : t + 1]
@@ -132,18 +137,22 @@ def tile_sub_graph_pa_kernel(tc, x_nodes, w1, b1, gamma, beta, w2, b2, out):
         def b2_col(c):
             return b2_cols[:, c : c + 1]
 
-        def quantise_weight(raw, width, label, permute):
-            grouped = const.tile([P, width, PACK], BF16, align_bytes=64, name=label + "_grouped")
-            if permute:
-                nc.vector.tensor_copy(
-                    out=grouped[:].rearrange("p (t m) j -> p t m j", t=PACK),
-                    in_=raw[:].rearrange("p j (m t) -> p t m j", t=PACK),
-                )
-            else:
-                nc.vector.tensor_copy(
-                    out=grouped[:].rearrange("p (c i) t -> p c t i", i=RUN),
-                    in_=raw[:].rearrange("p t (c i) -> p c t i", i=RUN),
-                )
+        w1_grouped = const.tile([P, H, PACK], BF16, align_bytes=64)
+        w2_grouped = const.tile([P, G, PACK], BF16, align_bytes=64)
+
+        def regroup_w1():
+            nc.vector.tensor_copy(
+                out=w1_grouped[:].rearrange("p (t m) j -> p t m j", t=PACK),
+                in_=w1_raw[:].rearrange("p j (m t) -> p t m j", t=PACK),
+            )
+
+        def regroup_w2():
+            nc.vector.tensor_copy(
+                out=w2_grouped[:].rearrange("p (c i) j -> p c j i", i=RUN),
+                in_=w2_raw[:].rearrange("p j (c i) -> p c j i", i=RUN),
+            )
+
+        def quantise_weight(grouped, width, label):
             codes = const.tile([P, width], U32, align_bytes=64, name=label + "_codes")
             scales = const.tile([P, width], U8, align_bytes=64, name=label + "_scales")
             nc.vector.quantize_mx(
@@ -153,7 +162,8 @@ def tile_sub_graph_pa_kernel(tc, x_nodes, w1, b1, gamma, beta, w2, b2, out):
             )
             return codes, scales
 
-        w1_codes, w1_scales = quantise_weight(w1_raw, H, "w1", True)
+        regroup_w1()
+        w1_codes, w1_scales = quantise_weight(w1_grouped, H, "w1")
         w2_q = {}
 
         live = {}
@@ -162,8 +172,8 @@ def tile_sub_graph_pa_kernel(tc, x_nodes, w1, b1, gamma, beta, w2, b2, out):
         def transpose_x(unit):
             if unit not in units:
                 return
-            xt_ps = psum_x.tile([P, TILES, 2, P], F32)
-            for j in range(TILES):
+            xt_ps = psum_x.tile([P, UNIT_TILES[unit], 2, P], F32, tag="x_ps")
+            for j in range(UNIT_TILES[unit]):
                 words = x_tiles[unit][:, j, :].bitcast(F32)
                 for u in range(2):
                     nc.tensor.transpose(xt_ps[:, j, u, :], words[:, u::2], ident[:])
@@ -172,22 +182,28 @@ def tile_sub_graph_pa_kernel(tc, x_nodes, w1, b1, gamma, beta, w2, b2, out):
         def copy_x(unit):
             if unit not in units:
                 return
-            x_words = per_unit.tile([P, TILES, P, 2], F32, align_bytes=64)
+            x_words = per_unit.tile([P, UNIT_TILES[unit], P, 2], F32, align_bytes=64)
             nc.scalar.copy(out=x_words[:], in_=live.pop(("xt_ps", unit))[:].rearrange("p j u r -> p j r u"))
             live["x_words", unit] = x_words
 
-        def first_matmul(unit):
+        def quantise_x(unit):
             if unit not in units:
                 return
             x_words = live.pop(("x_words", unit))
-            x_codes = per_unit.tile([P, UNIT], U32, align_bytes=64)
-            x_scales = per_unit.tile([P, UNIT], U8, align_bytes=64)
+            x_codes = per_unit.tile([P, UNIT_TILES[unit] * P], U32, align_bytes=64)
+            x_scales = per_unit.tile([P, UNIT_TILES[unit] * P], U8, align_bytes=64)
             nc.vector.quantize_mx(
                 out=x_codes[:].bitcast(FP8X4),
                 scales=x_scales[:],
                 in_=x_words[:].rearrange("p j r u -> p (j r u)").bitcast(BF16),
             )
-            for j in range(TILES):
+            live["x_q", unit] = x_codes, x_scales
+
+        def first_matmul(unit):
+            if unit not in units:
+                return
+            x_codes, x_scales = live.pop(("x_q", unit))
+            for j in range(UNIT_TILES[unit]):
                 tokens = slice(j * P, (j + 1) * P)
                 h_ps = psum_h.tile([P, H], F32, tag="h_ps")
                 nc.tensor.matmul_mx(
@@ -204,10 +220,10 @@ def tile_sub_graph_pa_kernel(tc, x_nodes, w1, b1, gamma, beta, w2, b2, out):
         def bias_and_squares(unit):
             if unit not in units:
                 return
-            h_sum = per_unit.tile([P, TILES], F32)
-            sq_sum = per_unit.tile([P, TILES], F32)
+            h_sum = per_unit.tile([P, UNIT_TILES[unit]], F32)
+            sq_sum = per_unit.tile([P, UNIT_TILES[unit]], F32)
             h_tiles = []
-            for j in range(TILES):
+            for j in range(UNIT_TILES[unit]):
                 h = per_tile.tile([P, H], F32)
                 nc.vector.scalar_tensor_tensor(
                     out=h[:],
@@ -219,7 +235,7 @@ def tile_sub_graph_pa_kernel(tc, x_nodes, w1, b1, gamma, beta, w2, b2, out):
                     accum_out=h_sum[:, j : j + 1],
                 )
                 h_tiles.append(h)
-            for j in range(TILES):
+            for j in range(UNIT_TILES[unit]):
                 squares = per_tile.tile([P, H], BF16)
                 nc.scalar.activation(
                     out=squares[:],
@@ -239,13 +255,13 @@ def tile_sub_graph_pa_kernel(tc, x_nodes, w1, b1, gamma, beta, w2, b2, out):
             h_tiles = live.pop(("h", unit))
             h_sum = live.pop(("h_sum", unit))
             sq_sum = live.pop(("sq_sum", unit))
-            neg_mean = per_unit.tile([P, TILES], F32)
+            neg_mean = per_unit.tile([P, UNIT_TILES[unit]], F32)
             nc.scalar.mul(out=neg_mean[:], in_=h_sum[:], mul=-1.0 / H)
-            rstd = per_unit.tile([P, TILES], F32)
+            rstd = per_unit.tile([P, UNIT_TILES[unit]], F32)
             nc.scalar.activation(
                 out=rstd[:], in_=sq_sum[:], func=ACT.Abs_reciprocal_sqrt, bias=eps[:], scale=1.0 / (H * H * H)
             )
-            for j in range(TILES):
+            for j in range(UNIT_TILES[unit]):
                 z = per_tile.tile([P, H], F32)
                 nc.gpsimd.tensor_scalar(
                     out=z[:],
@@ -260,13 +276,13 @@ def tile_sub_graph_pa_kernel(tc, x_nodes, w1, b1, gamma, beta, w2, b2, out):
         def to_features(unit):
             if unit not in units:
                 return
-            z_tiles = [live.pop(("z", unit, j)) for j in range(TILES)]
-            r_planes = per_unit.tile([P, PACK, UNIT], BF16)
+            z_tiles = [live.pop(("z", unit, j)) for j in range(UNIT_TILES[unit])]
+            r_planes = per_unit.tile([P, PACK, UNIT_TILES[unit] * P], BF16)
             z_banks = []
             for pair in range(PACK // 2):
-                z_ps = psum_z.tile([P, 2, UNIT], F32)
+                z_ps = psum_z.tile([P, 2, UNIT_TILES[unit] * P], F32)
                 z_banks.append(z_ps)
-            for j in range(TILES):
+            for j in range(UNIT_TILES[unit]):
                 for t in range(PACK):
                     nc.tensor.transpose(
                         z_banks[t // 2][:, t % 2, j * P : (j + 1) * P], z_tiles[j][:, t * P : (t + 1) * P], ident[:]
@@ -285,7 +301,7 @@ def tile_sub_graph_pa_kernel(tc, x_nodes, w1, b1, gamma, beta, w2, b2, out):
             if unit not in units:
                 return
             r_planes = live.pop(("r_planes", unit))
-            r_grouped = per_unit.tile([P, UNIT, PACK], BF16, align_bytes=64)
+            r_grouped = per_unit.tile([P, UNIT_TILES[unit] * P, PACK], BF16, align_bytes=64)
             nc.vector.tensor_copy(
                 out=r_grouped[:].rearrange("p (c i) t -> p c t i", i=RUN),
                 in_=r_planes[:].rearrange("p t (c i) -> p c t i", i=RUN),
@@ -296,8 +312,8 @@ def tile_sub_graph_pa_kernel(tc, x_nodes, w1, b1, gamma, beta, w2, b2, out):
             if unit not in units:
                 return
             r_grouped = live.pop(("r_grouped", unit))
-            r_codes = per_unit.tile([P, UNIT], U32, align_bytes=64)
-            r_scales = per_unit.tile([P, UNIT], U8, align_bytes=64)
+            r_codes = per_unit.tile([P, UNIT_TILES[unit] * P], U32, align_bytes=64)
+            r_scales = per_unit.tile([P, UNIT_TILES[unit] * P], U8, align_bytes=64)
             nc.vector.quantize_mx(
                 out=r_codes[:].bitcast(FP8X4),
                 scales=r_scales[:],
@@ -312,8 +328,8 @@ def tile_sub_graph_pa_kernel(tc, x_nodes, w1, b1, gamma, beta, w2, b2, out):
             r_codes = live.pop(("r_codes", unit))
             r_scales = live.pop(("r_scales", unit))
             w2_codes, w2_scales = w2_q["codes"], w2_q["scales"]
-            x1_ps = psum_a.tile([P, TILES, G], F32, tag="x1_ps")
-            for j in range(TILES):
+            x1_ps = psum_a.tile([P, UNIT_TILES[unit], G], F32, tag="x1_ps")
+            for j in range(UNIT_TILES[unit]):
                 tokens = slice(j * P, (j + 1) * P)
                 nc.tensor.matmul_mx(
                     out=x1_ps[:, j, :],
@@ -324,7 +340,7 @@ def tile_sub_graph_pa_kernel(tc, x_nodes, w1, b1, gamma, beta, w2, b2, out):
                     start=True,
                     stop=True,
                 )
-            x1t_ps = psum_b.tile([P, HALVES, UNIT], F32, tag="x1t_ps")
+            x1t_ps = psum_b.tile([P, HALVES, UNIT_TILES[unit] * P], F32, tag="x1t_ps")
             for c in range(HALVES):
                 channels = slice(c * P, (c + 1) * P)
                 nc.tensor.matmul_mx(
@@ -339,53 +355,67 @@ def tile_sub_graph_pa_kernel(tc, x_nodes, w1, b1, gamma, beta, w2, b2, out):
             live["x1_ps", unit] = x1_ps
             live["x1t_ps", unit] = x1t_ps
 
+        def group_of(unit):
+            g = max(n for n in range(len(GROUP_TILES)) if GROUP_START[n] <= UNIT_START[unit])
+            return g, UNIT_START[unit] - GROUP_START[g]
+
+        def closed_group(unit):
+            if unit not in units:
+                return None
+            g, tile_in_group = group_of(unit)
+            return g if tile_in_group + UNIT_TILES[unit] == GROUP_TILES[g] else None
+
         def outputs(unit):
             if unit not in units:
                 return
-            g, part = divmod(unit, UNITS_PER_GROUP)
-            x1 = per_unit.tile([P, TILES, G], F32)
+            x1 = per_unit.tile([P, UNIT_TILES[unit], G], F32)
             nc.vector.tensor_tensor(
                 out=x1[:],
                 in0=live.pop(("x1_ps", unit))[:],
-                in1=b2_rows[:].unsqueeze(1).to_broadcast([P, TILES, G]),
+                in1=b2_rows[:].unsqueeze(1).to_broadcast([P, UNIT_TILES[unit], G]),
                 op=ALU.add,
             )
             nc.sync.dma_start(
-                out=out_flat[unit * UNIT : (unit + 1) * UNIT, 0:G].rearrange("(j p) c -> p j c", p=P),
+                out=out_flat[rows_of(unit), 0:G].rearrange("(j p) c -> p j c", p=P),
                 in_=x1[:],
             )
-            if part == 0:
-                pooled_new = per_unit.tile([P, HALVES, LINES_PER_GROUP], F32)
+            g, tile_in_group = group_of(unit)
+            if tile_in_group == 0:
+                pooled_new = per_unit.tile([P, HALVES, GROUP_TILES[g] * LINES_PER_TILE], F32)
                 live["pooled", g] = pooled_new
-            pooled = live["pooled", g]
+            first_line = tile_in_group * LINES_PER_TILE
             nc.vector.tensor_reduce(
-                out=pooled[:, :, part * LINES_PER_UNIT : (part + 1) * LINES_PER_UNIT],
+                out=live["pooled", g][:, :, first_line : first_line + UNIT_TILES[unit] * LINES_PER_TILE],
                 in_=live.pop(("x1t_ps", unit))[:].rearrange("p c (b l) -> p c b l", l=NODES),
                 axis=AXIS.X,
                 op=ALU.max,
             )
 
         def spread_maxima(unit):
-            g, part = divmod(unit, UNITS_PER_GROUP)
-            if unit not in units or part < UNITS_PER_GROUP - 1:
+            g = closed_group(unit)
+            if g is None:
                 return
+            lines = GROUP_TILES[g] * LINES_PER_TILE
+            copies = P // lines
             pooled = live.pop(("pooled", g))
-            spread = per_unit.tile([P, HALVES, LINES_PER_GROUP, COPIES], F32)
+            spread = per_unit.tile([P, HALVES, lines, copies], F32)
             for c in range(HALVES):
                 nc.scalar.activation(
                     out=spread[:, c, :, :],
-                    in_=pooled[:, c, :].unsqueeze(2).to_broadcast([P, LINES_PER_GROUP, COPIES]),
+                    in_=pooled[:, c, :].unsqueeze(2).to_broadcast([P, lines, copies]),
                     func=ACT.Identity,
                     bias=b2_col(c),
                 )
             live["spread", g] = spread
 
         def pool(unit):
-            g, part = divmod(unit, UNITS_PER_GROUP)
-            if unit not in units or part < UNITS_PER_GROUP - 1:
+            g = closed_group(unit)
+            if g is None:
                 return
+            lines = GROUP_TILES[g] * LINES_PER_TILE
+            copies = P // lines
             spread = live.pop(("spread", g))
-            x2_ps = psum_s.tile([P, G], F32, tag="small")
+            x2_ps = psum_x.tile([P, G], F32, tag="x_ps")
             for c in range(HALVES):
                 nc.tensor.transpose(
                     x2_ps[:, c * P : (c + 1) * P],
@@ -395,10 +425,10 @@ def tile_sub_graph_pa_kernel(tc, x_nodes, w1, b1, gamma, beta, w2, b2, out):
             x2 = per_unit.tile([P, G], F32)
             nc.scalar.copy(out=x2[:], in_=x2_ps[:])
             nc.sync.dma_start(
-                out=out_flat[g * GROUP : (g + 1) * GROUP, G : 2 * G].rearrange(
-                    "(q i) c -> q i c", i=ROWS_PER_COPY
+                out=out_flat[GROUP_START[g] * P : (GROUP_START[g] + GROUP_TILES[g]) * P, G : 2 * G].rearrange(
+                    "(q i) c -> q i c", i=NODES // copies
                 ),
-                in_=x2[:].unsqueeze(1).to_broadcast([P, ROWS_PER_COPY, G]),
+                in_=x2[:].unsqueeze(1).to_broadcast([P, NODES // copies, G]),
             )
 
         for k in range(N_UNITS + S_POOL):
@@ -411,10 +441,15 @@ def tile_sub_graph_pa_kernel(tc, x_nodes, w1, b1, gamma, beta, w2, b2, out):
             to_features(k - S_FEATURES)
             regroup_r(k - S_QUANTISE_R)
             first_matmul(k - S_FIRST)
+            quantise_x(k - S_QUANTISE_X)
             pool(k - S_POOL)
             quantise_r(k - S_QUANTISE_R)
-            transpose_x(k - S_TRANSPOSE_X)
             if k == S_COPY_X:
-                spread_constants()
-            if k == S_FEATURES:
-                w2_q["codes"], w2_q["scales"] = quantise_weight(w2_raw, G, "w2", False)
+                spread_b1()
+            transpose_x(k - S_TRANSPOSE_X)
+            if k == S_FIRST:
+                regroup_w2()
+            if k == S_NORM:
+                nc.vector.tensor_copy(out=affine[:], in_=affine_bf[:, :, 0:PACK])
+                w2_q["codes"], w2_q["scales"] = quantise_weight(w2_grouped, G, "w2")
+                spread_b2()

@@ -23,7 +23,7 @@ EPS = 1e-5
 TILES = TOKENS // P
 LINES_PER_TILE = P // NODES
 UNIT_TILES = (1, 1) + 14 * (2,) + (1, 1)
-GROUP_TILES = 8 * (4,)
+GROUP_TILES = (16, 8, 4, 2, 2)
 HALVES = G // P
 RUN = 4
 
@@ -89,9 +89,10 @@ def tile_sub_graph_pa_kernel(tc, x_nodes, w1, b1, gamma, beta, w2, b2, out):
         nc.scalar.dma_start(out=affine_bf[:, 1, 0:PACK], in_=beta.rearrange("(p t) -> p t", t=PACK))
 
         load_x(1)
+        load_x(2)
         w2_raw = const.tile([P, PACK, G], BF16)
         nc.sync.dma_start(out=w2_raw[:], in_=w2.rearrange("(p j) n -> p j n", j=PACK))
-        for unit in range(2, N_UNITS):
+        for unit in range(3, N_UNITS):
             load_x(unit)
 
         ident = const.tile([P, P], F32)
@@ -328,18 +329,6 @@ def tile_sub_graph_pa_kernel(tc, x_nodes, w1, b1, gamma, beta, w2, b2, out):
             r_codes = live.pop(("r_codes", unit))
             r_scales = live.pop(("r_scales", unit))
             w2_codes, w2_scales = w2_q["codes"], w2_q["scales"]
-            x1_ps = psum_a.tile([P, UNIT_TILES[unit], G], F32, tag="x1_ps")
-            for j in range(UNIT_TILES[unit]):
-                tokens = slice(j * P, (j + 1) * P)
-                nc.tensor.matmul_mx(
-                    out=x1_ps[:, j, :],
-                    lhsT=r_codes[:, tokens].bitcast(FP8X4),
-                    lhsT_scale=r_scales[:, tokens],
-                    rhs=w2_codes[:].bitcast(FP8X4),
-                    rhs_scale=w2_scales[:],
-                    start=True,
-                    stop=True,
-                )
             x1t_ps = psum_b.tile([P, HALVES, UNIT_TILES[unit] * P], F32, tag="x1t_ps")
             for c in range(HALVES):
                 channels = slice(c * P, (c + 1) * P)
@@ -349,6 +338,18 @@ def tile_sub_graph_pa_kernel(tc, x_nodes, w1, b1, gamma, beta, w2, b2, out):
                     lhsT_scale=w2_scales[:, channels],
                     rhs=r_codes[:].bitcast(FP8X4),
                     rhs_scale=r_scales[:],
+                    start=True,
+                    stop=True,
+                )
+            x1_ps = psum_a.tile([P, UNIT_TILES[unit], G], F32, tag="x1_ps")
+            for j in range(UNIT_TILES[unit]):
+                tokens = slice(j * P, (j + 1) * P)
+                nc.tensor.matmul_mx(
+                    out=x1_ps[:, j, :],
+                    lhsT=r_codes[:, tokens].bitcast(FP8X4),
+                    lhsT_scale=r_scales[:, tokens],
+                    rhs=w2_codes[:].bitcast(FP8X4),
+                    rhs_scale=w2_scales[:],
                     start=True,
                     stop=True,
                 )
@@ -368,17 +369,6 @@ def tile_sub_graph_pa_kernel(tc, x_nodes, w1, b1, gamma, beta, w2, b2, out):
         def outputs(unit):
             if unit not in units:
                 return
-            x1 = per_unit.tile([P, UNIT_TILES[unit], G], F32)
-            nc.vector.tensor_tensor(
-                out=x1[:],
-                in0=live.pop(("x1_ps", unit))[:],
-                in1=b2_rows[:].unsqueeze(1).to_broadcast([P, UNIT_TILES[unit], G]),
-                op=ALU.add,
-            )
-            nc.sync.dma_start(
-                out=out_flat[rows_of(unit), 0:G].rearrange("(j p) c -> p j c", p=P),
-                in_=x1[:],
-            )
             g, tile_in_group = group_of(unit)
             if tile_in_group == 0:
                 pooled_new = per_unit.tile([P, HALVES, GROUP_TILES[g] * LINES_PER_TILE], F32)
@@ -389,6 +379,17 @@ def tile_sub_graph_pa_kernel(tc, x_nodes, w1, b1, gamma, beta, w2, b2, out):
                 in_=live.pop(("x1t_ps", unit))[:].rearrange("p c (b l) -> p c b l", l=NODES),
                 axis=AXIS.X,
                 op=ALU.max,
+            )
+            x1 = per_unit.tile([P, UNIT_TILES[unit], G], F32)
+            nc.vector.tensor_tensor(
+                out=x1[:],
+                in0=live.pop(("x1_ps", unit))[:],
+                in1=b2_rows[:].unsqueeze(1).to_broadcast([P, UNIT_TILES[unit], G]),
+                op=ALU.add,
+            )
+            nc.sync.dma_start(
+                out=out_flat[rows_of(unit), 0:G].rearrange("(j p) c -> p j c", p=P),
+                in_=x1[:],
             )
 
         def spread_maxima(unit):

@@ -33,10 +33,13 @@ S_QUANTISE_X = 2
 S_FIRST = 3
 S_NORM = 4
 S_FEATURES = 6
-S_QUANTISE_R = 7
-S_SECOND = 8
-S_OUTPUTS = 9
-S_POOL = 10
+S_REGROUP = 7
+S_QUANTISE_R = 8
+S_SECOND = 9
+S_OUTPUTS = 10
+S_POOL = 11
+
+FULL = 4
 
 N_UNITS = len(UNIT_TILES)
 UNIT_START = [sum(UNIT_TILES[:n]) for n in range(N_UNITS)]
@@ -104,6 +107,8 @@ def tile_sub_graph_pa_kernel(tc, x_nodes, w1, b1, gamma, beta, w2, b2, out):
         warm = const.tile([P, 1], F32)
         nc.scalar.activation(out=warm[:], in_=eps[:], func=ACT.Abs_reciprocal_sqrt)
 
+        ident_bf = const.tile([P, P], BF16)
+        nc.vector.tensor_copy(out=ident_bf[:], in_=ident[:])
         affine = const.tile([P, 2, PACK], F32)
         b2_cols = const.tile([P, HALVES], F32)
         b1_rows = const.tile([P, H], F32)
@@ -302,12 +307,38 @@ def tile_sub_graph_pa_kernel(tc, x_nodes, w1, b1, gamma, beta, w2, b2, out):
             if unit not in units:
                 return
             r_planes = live.pop(("r_planes", unit))
+            r_grouped = live["r_grouped", unit]
+            if by_vector(unit) > 0:
+                tokens = slice(0, by_vector(unit) * P)
+                nc.vector.tensor_copy(
+                    out=r_grouped[:, tokens, :].rearrange("p (c i) t -> p c t i", i=RUN),
+                    in_=r_planes[:, :, tokens].rearrange("p t (c i) -> p c t i", i=RUN),
+                )
+
+        def by_vector(unit):
+            return UNIT_TILES[unit] if unit < FULL else 1
+
+        def regroup_by_tensor(unit):
+            if unit not in units:
+                return
             r_grouped = per_unit.tile([P, UNIT_TILES[unit] * P, PACK], BF16, align_bytes=64)
-            nc.vector.tensor_copy(
-                out=r_grouped[:].rearrange("p (c i) t -> p c t i", i=RUN),
-                in_=r_planes[:].rearrange("p t (c i) -> p c t i", i=RUN),
-            )
             live["r_grouped", unit] = r_grouped
+            for j in range(by_vector(unit), UNIT_TILES[unit]):
+                rg_ps = psum_x.tile([P, P, PACK], BF16, tag="x_ps")
+                nc.tensor.matmul(
+                    out=rg_ps[:].rearrange("p r t -> p (r t)"),
+                    lhsT=ident_bf[:],
+                    rhs=live["r_planes", unit][:, :, j * P : (j + 1) * P].rearrange("p t r -> p r t"),
+                    start=True,
+                    stop=True,
+                )
+                live["rg_ps", unit, j] = rg_ps
+
+        def copy_regrouped(unit):
+            if unit not in units:
+                return
+            for j in range(by_vector(unit), UNIT_TILES[unit]):
+                nc.scalar.copy(out=live["r_grouped", unit][:, j * P : (j + 1) * P, :], in_=live.pop(("rg_ps", unit, j))[:])
 
         def quantise_r(unit):
             if unit not in units:
@@ -440,7 +471,9 @@ def tile_sub_graph_pa_kernel(tc, x_nodes, w1, b1, gamma, beta, w2, b2, out):
             copy_x(k - S_COPY_X)
             normalise(k - S_NORM)
             to_features(k - S_FEATURES)
-            regroup_r(k - S_QUANTISE_R)
+            regroup_by_tensor(k - S_REGROUP)
+            copy_regrouped(k - S_REGROUP)
+            regroup_r(k - S_REGROUP)
             first_matmul(k - S_FIRST)
             quantise_x(k - S_QUANTISE_X)
             pool(k - S_POOL)

@@ -39,6 +39,7 @@ S_SECOND = 9
 S_OUTPUTS = 10
 S_POOL = 11
 
+X_BY_VECTOR = range(5, 8)
 FULL = 4
 
 N_UNITS = len(UNIT_TILES)
@@ -58,6 +59,7 @@ def tile_sub_graph_pa_kernel(tc, x_nodes, w1, b1, gamma, beta, w2, b2, out):
         const = ctx.enter_context(tc.tile_pool(name="const", bufs=1))
         per_unit = ctx.enter_context(tc.tile_pool(name="per_unit", bufs=4))
         per_tile = ctx.enter_context(tc.tile_pool(name="per_tile", bufs=8))
+        stores = ctx.enter_context(tc.tile_pool(name="stores", bufs=8))
         psum_x = ctx.enter_context(tc.psum_pool(name="psum_x", bufs=2))
         psum_h = ctx.enter_context(tc.psum_pool(name="psum_h", bufs=2))
         psum_z = ctx.enter_context(tc.psum_pool(name="psum_z", bufs=2))
@@ -147,10 +149,12 @@ def tile_sub_graph_pa_kernel(tc, x_nodes, w1, b1, gamma, beta, w2, b2, out):
         w2_grouped = const.tile([P, G, PACK], BF16, align_bytes=64)
 
         def regroup_w1():
-            nc.vector.tensor_copy(
-                out=w1_grouped[:].rearrange("p (t m) j -> p t m j", t=PACK),
-                in_=w1_raw[:].rearrange("p j (m t) -> p t m j", t=PACK),
-            )
+            for t in range(PACK):
+                copy = nc.scalar.copy if t == PACK - 1 else nc.vector.tensor_copy
+                copy(
+                    out=w1_grouped[:, t * P : (t + 1) * P, :],
+                    in_=w1_raw[:, :, t::PACK].rearrange("p j m -> p m j"),
+                )
 
         def regroup_w2():
             nc.vector.tensor_copy(
@@ -161,11 +165,12 @@ def tile_sub_graph_pa_kernel(tc, x_nodes, w1, b1, gamma, beta, w2, b2, out):
         def quantise_weight(grouped, width, label):
             codes = const.tile([P, width], U32, align_bytes=64, name=label + "_codes")
             scales = const.tile([P, width], U8, align_bytes=64, name=label + "_scales")
-            nc.vector.quantize_mx(
-                out=codes[:].bitcast(FP8X4),
-                scales=scales[:],
-                in_=grouped[:].rearrange("p c t -> p (c t)"),
-            )
+            for c in range(0, width, 256):
+                nc.vector.quantize_mx(
+                    out=codes[:, c : c + 256].bitcast(FP8X4),
+                    scales=scales[:, c : c + 256],
+                    in_=grouped[:, c : c + 256, :].rearrange("p c t -> p (c t)"),
+                )
             return codes, scales
 
         regroup_w1()
@@ -178,7 +183,10 @@ def tile_sub_graph_pa_kernel(tc, x_nodes, w1, b1, gamma, beta, w2, b2, out):
         def transpose_x(unit):
             if unit not in units:
                 return
-            xt_ps = psum_x.tile([P, UNIT_TILES[unit], 2, P], F32, tag="x_ps")
+            if unit == 2:
+                xt_ps = psum_z.tile([P, UNIT_TILES[unit], 2, P], F32, tag="z_ps")
+            else:
+                xt_ps = psum_x.tile([P, UNIT_TILES[unit], 2, P], F32, tag="x_ps")
             for j in range(UNIT_TILES[unit]):
                 words = x_tiles[unit][:, j, :].bitcast(F32)
                 for u in range(2):
@@ -189,7 +197,8 @@ def tile_sub_graph_pa_kernel(tc, x_nodes, w1, b1, gamma, beta, w2, b2, out):
             if unit not in units:
                 return
             x_words = per_unit.tile([P, UNIT_TILES[unit], P, 2], F32, align_bytes=64)
-            nc.scalar.copy(out=x_words[:], in_=live.pop(("xt_ps", unit))[:].rearrange("p j u r -> p j r u"))
+            copy = nc.vector.tensor_copy if unit in X_BY_VECTOR else nc.scalar.copy
+            copy(out=x_words[:], in_=live.pop(("xt_ps", unit))[:].rearrange("p j u r -> p j r u"))
             live["x_words", unit] = x_words
 
         def quantise_x(unit):
@@ -286,7 +295,7 @@ def tile_sub_graph_pa_kernel(tc, x_nodes, w1, b1, gamma, beta, w2, b2, out):
             r_planes = per_unit.tile([P, PACK, UNIT_TILES[unit] * P], BF16)
             z_banks = []
             for pair in range(PACK // 2):
-                z_ps = psum_z.tile([P, 2, UNIT_TILES[unit] * P], F32)
+                z_ps = psum_z.tile([P, 2, UNIT_TILES[unit] * P], F32, tag="z_ps")
                 z_banks.append(z_ps)
             for j in range(UNIT_TILES[unit]):
                 for t in range(PACK):
@@ -411,7 +420,7 @@ def tile_sub_graph_pa_kernel(tc, x_nodes, w1, b1, gamma, beta, w2, b2, out):
                 axis=AXIS.X,
                 op=ALU.max,
             )
-            x1 = per_unit.tile([P, UNIT_TILES[unit], G], F32)
+            x1 = stores.tile([P, UNIT_TILES[unit], G], F32)
             nc.vector.tensor_tensor(
                 out=x1[:],
                 in0=live.pop(("x1_ps", unit))[:],
@@ -466,24 +475,31 @@ def tile_sub_graph_pa_kernel(tc, x_nodes, w1, b1, gamma, beta, w2, b2, out):
         for k in range(N_UNITS + S_POOL):
             spread_maxima(k - S_POOL)
             outputs(k - S_OUTPUTS)
+            draining = k - S_NORM >= N_UNITS
+            if draining:
+                to_features(k - S_FEATURES)
+                pool(k - S_POOL)
             second_matmuls(k - S_SECOND)
             bias_and_squares(k - S_NORM)
             copy_x(k - S_COPY_X)
             normalise(k - S_NORM)
-            to_features(k - S_FEATURES)
+            if not draining:
+                to_features(k - S_FEATURES)
             regroup_by_tensor(k - S_REGROUP)
             copy_regrouped(k - S_REGROUP)
             regroup_r(k - S_REGROUP)
             first_matmul(k - S_FIRST)
             quantise_x(k - S_QUANTISE_X)
-            pool(k - S_POOL)
+            if not draining:
+                pool(k - S_POOL)
             quantise_r(k - S_QUANTISE_R)
+            if k == S_QUANTISE_X:
+                regroup_w2()
+            if k == S_FIRST:
+                spread_b2()
             if k == S_COPY_X:
                 spread_b1()
             transpose_x(k - S_TRANSPOSE_X)
-            if k == S_FIRST:
-                regroup_w2()
             if k == S_NORM:
                 nc.vector.tensor_copy(out=affine[:], in_=affine_bf[:, :, 0:PACK])
                 w2_q["codes"], w2_q["scales"] = quantise_weight(w2_grouped, G, "w2")
-                spread_b2()

@@ -264,18 +264,24 @@ def tile_sub_graph_pa_kernel(tc, x_nodes, w1, b1, gamma, beta, w2, b2, out):
             live["h_sum", unit] = h_sum
             live["sq_sum", unit] = sq_sum
 
+        def inverse_deviation(unit):
+            if unit not in units:
+                return
+            sq_sum = live.pop(("sq_sum", unit))
+            rstd = per_unit.tile([P, UNIT_TILES[unit]], F32)
+            nc.scalar.activation(
+                out=rstd[:], in_=sq_sum[:], func=ACT.Abs_reciprocal_sqrt, bias=eps[:], scale=1.0 / (H * H * H)
+            )
+            live["rstd", unit] = rstd
+
         def normalise(unit):
             if unit not in units:
                 return
             h_tiles = live.pop(("h", unit))
             h_sum = live.pop(("h_sum", unit))
-            sq_sum = live.pop(("sq_sum", unit))
+            rstd = live.pop(("rstd", unit))
             neg_mean = per_unit.tile([P, UNIT_TILES[unit]], F32)
-            nc.scalar.mul(out=neg_mean[:], in_=h_sum[:], mul=-1.0 / H)
-            rstd = per_unit.tile([P, UNIT_TILES[unit]], F32)
-            nc.scalar.activation(
-                out=rstd[:], in_=sq_sum[:], func=ACT.Abs_reciprocal_sqrt, bias=eps[:], scale=1.0 / (H * H * H)
-            )
+            nc.vector.tensor_scalar(out=neg_mean[:], in0=h_sum[:], scalar1=-1.0 / H, scalar2=None, op0=ALU.mult)
             for j in range(UNIT_TILES[unit]):
                 z = per_tile.tile([P, H], F32)
                 nc.gpsimd.tensor_scalar(
@@ -474,25 +480,28 @@ def tile_sub_graph_pa_kernel(tc, x_nodes, w1, b1, gamma, beta, w2, b2, out):
 
         for k in range(N_UNITS + S_POOL):
             spread_maxima(k - S_POOL)
+            bias_and_squares(k - S_NORM)
             outputs(k - S_OUTPUTS)
             draining = k - S_NORM >= N_UNITS
             if draining:
                 to_features(k - S_FEATURES)
                 pool(k - S_POOL)
-            second_matmuls(k - S_SECOND)
-            bias_and_squares(k - S_NORM)
+                second_matmuls(k - S_SECOND)
             copy_x(k - S_COPY_X)
-            normalise(k - S_NORM)
+            inverse_deviation(k - S_NORM)
             if not draining:
                 to_features(k - S_FEATURES)
             regroup_by_tensor(k - S_REGROUP)
             copy_regrouped(k - S_REGROUP)
             regroup_r(k - S_REGROUP)
             first_matmul(k - S_FIRST)
+            if not draining:
+                second_matmuls(k - S_SECOND)
             quantise_x(k - S_QUANTISE_X)
             if not draining:
                 pool(k - S_POOL)
             quantise_r(k - S_QUANTISE_R)
+            normalise(k - S_NORM)
             if k == S_QUANTISE_X:
                 regroup_w2()
             if k == S_FIRST:

from contextlib import ExitStack

import concourse.mybir as mybir
from concourse.masks import make_identity

F32 = mybir.dt.float32
BF16 = mybir.dt.bfloat16
U32 = mybir.dt.uint32
U8 = mybir.dt.uint8
FP8X4 = mybir.dt.float8_e4m3fn_x4
ALU = mybir.AluOpType
ACT = mybir.ActivationFunctionType
AXIS = mybir.AxisListType

P = 128
PACK = 4
TOKENS = 64 * 64
NODES = 64
H = 512
G = 256
EPS = 1e-5

TILES = TOKENS // P
LINES_PER_TILE = P // NODES
UNIT_TILES = (1, 1) + 14 * (2,) + (1, 1)
GROUP_TILES = (16, 8, 4, 2, 2)
HALVES = G // P
RUN = 4

S_TRANSPOSE_X = 0
S_COPY_X = 1
S_QUANTISE_X = 2
S_FIRST = 3
S_NORM = 4
S_FEATURES = 6
S_REGROUP = 7
S_QUANTISE_R = 8
S_SECOND = 9
S_OUTPUTS = 10
S_POOL = 11

X_BY_VECTOR = range(5, 8)
FULL = 4

N_UNITS = len(UNIT_TILES)
UNIT_START = [sum(UNIT_TILES[:n]) for n in range(N_UNITS)]
GROUP_START = [sum(GROUP_TILES[:n]) for n in range(len(GROUP_TILES))]

FLOPS = 2 * TOKENS * H * H + 2 * TOKENS * H * G


def tile_sub_graph_pa_kernel(tc, x_nodes, w1, b1, gamma, beta, w2, b2, out):
    nc = tc.nc
    x_flat = x_nodes.flatten_outer_dims()
    out_flat = out.flatten_outer_dims()

    with ExitStack() as ctx:
        ctx.enter_context(tc.manual_schedule())
        const = ctx.enter_context(tc.tile_pool(name="const", bufs=1))
        per_unit = ctx.enter_context(tc.tile_pool(name="per_unit", bufs=4))
        per_tile = ctx.enter_context(tc.tile_pool(name="per_tile", bufs=8))
        stores = ctx.enter_context(tc.tile_pool(name="stores", bufs=8))
        psum_x = ctx.enter_context(tc.psum_pool(name="psum_x", bufs=2))
        psum_h = ctx.enter_context(tc.psum_pool(name="psum_h", bufs=2))
        psum_z = ctx.enter_context(tc.psum_pool(name="psum_z", bufs=2))
        psum_a = ctx.enter_context(tc.psum_pool(name="psum_a", bufs=1))
        psum_b = ctx.enter_context(tc.psum_pool(name="psum_b", bufs=1))

        w1_raw = const.tile([P, PACK, H], BF16)
        nc.sync.dma_start(out=w1_raw[:], in_=w1.rearrange("(p j) c -> p j c", j=PACK))
        x_tiles = []
        for unit in range(N_UNITS):
            x_sb = const.tile([P, UNIT_TILES[unit], H], BF16, name="x_sb%d" % unit)
            x_tiles.append(x_sb)

        def rows_of(unit):
            start = UNIT_START[unit] * P
            return slice(start, start + UNIT_TILES[unit] * P)

        def load_x(unit):
            nc.sync.dma_start(
                out=x_tiles[unit][:],
                in_=x_flat[rows_of(unit), :].rearrange("(j p) k -> p j k", p=P),
            )

        load_x(0)

        bias_in = const.tile([P, H + G], BF16)
        nc.gpsimd.memset(bias_in[:].bitcast(F32), 0.0)
        nc.scalar.dma_start(out=bias_in[0:1, 0:H], in_=b1.rearrange("(o k) -> o k", o=1))
        nc.scalar.dma_start(out=bias_in[0:1, H : H + G], in_=b2.rearrange("(o k) -> o k", o=1))
        affine_bf = const.tile([P, 2, 16], BF16)
        nc.scalar.dma_start(out=affine_bf[:, 0, 0:PACK], in_=gamma.rearrange("(p t) -> p t", t=PACK))
        nc.scalar.dma_start(out=affine_bf[:, 1, 0:PACK], in_=beta.rearrange("(p t) -> p t", t=PACK))

        load_x(1)
        load_x(2)
        w2_raw = const.tile([P, PACK, G], BF16)
        nc.sync.dma_start(out=w2_raw[:], in_=w2.rearrange("(p j) n -> p j n", j=PACK))
        for unit in range(3, N_UNITS):
            load_x(unit)

        ident = const.tile([P, P], F32)
        make_identity(nc, ident[:])
        ones = const.tile([P, P], BF16)
        nc.vector.memset(ones[:], 1.0)
        eps = const.tile([P, 1], F32)
        nc.vector.memset(eps[:], EPS)
        warm = const.tile([P, 1], F32)
        nc.scalar.activation(out=warm[:], in_=eps[:], func=ACT.Abs_reciprocal_sqrt)

        ident_bf = const.tile([P, P], BF16)
        nc.vector.tensor_copy(out=ident_bf[:], in_=ident[:])
        affine = const.tile([P, 2, PACK], F32)
        b2_cols = const.tile([P, HALVES], F32)
        b1_rows = const.tile([P, H], F32)
        b2_rows = const.tile([P, G], F32)

        def spread_b1():
            b1_ps = psum_a.tile([P, H], F32, tag="x1_ps")
            nc.tensor.matmul(out=b1_ps[:], lhsT=ones[:], rhs=bias_in[:, 0:H], start=True, stop=True)
            nc.scalar.copy(
                out=b1_rows[:].rearrange("p (t m) -> p t m", t=PACK),
                in_=b1_ps[:].rearrange("p (m t) -> p t m", t=PACK),
            )

        def spread_b2():
            b2_ps = psum_b.tile([P, H], F32, tag="x1t_ps")
            nc.tensor.matmul(out=b2_ps[:, 0:G], lhsT=ones[:], rhs=bias_in[:, H : H + G], start=True, stop=True)
            nc.scalar.copy(out=b2_rows[:], in_=b2_ps[:, 0:G])
            cols_ps = psum_a.tile([P, H], F32, tag="x1_ps")
            for c in range(HALVES):
                channels = slice(H + c * P, H + (c + 1) * P)
                nc.tensor.matmul(
                    out=cols_ps[:, c : c + 1], lhsT=bias_in[:, channels], rhs=ones[:, 0:1], start=True, stop=True
                )
            nc.scalar.copy(out=b2_cols[:], in_=cols_ps[:, 0:HALVES])

        def gamma_col(t):
            return affine[:, 0, t : t + 1]

        def beta_col(t):
            return affine[:, 1, t : t + 1]

        def b2_col(c):
            return b2_cols[:, c : c + 1]

        w1_grouped = const.tile([P, H, PACK], BF16, align_bytes=64)
        w2_grouped = const.tile([P, G, PACK], BF16, align_bytes=64)

        def regroup_w1():
            for t in range(PACK):
                copy = nc.scalar.copy if t == PACK - 1 else nc.vector.tensor_copy
                copy(
                    out=w1_grouped[:, t * P : (t + 1) * P, :],
                    in_=w1_raw[:, :, t::PACK].rearrange("p j m -> p m j"),
                )

        def regroup_w2():
            nc.vector.tensor_copy(
                out=w2_grouped[:].rearrange("p (c i) j -> p c j i", i=RUN),
                in_=w2_raw[:].rearrange("p j (c i) -> p c j i", i=RUN),
            )

        def quantise_weight(grouped, width, label):
            codes = const.tile([P, width], U32, align_bytes=64, name=label + "_codes")
            scales = const.tile([P, width], U8, align_bytes=64, name=label + "_scales")
            for c in range(0, width, 256):
                nc.vector.quantize_mx(
                    out=codes[:, c : c + 256].bitcast(FP8X4),
                    scales=scales[:, c : c + 256],
                    in_=grouped[:, c : c + 256, :].rearrange("p c t -> p (c t)"),
                )
            return codes, scales

        regroup_w1()
        w1_codes, w1_scales = quantise_weight(w1_grouped, H, "w1")
        w2_q = {}

        live = {}
        units = range(N_UNITS)

        def transpose_x(unit):
            if unit not in units:
                return
            if unit == 2:
                xt_ps = psum_z.tile([P, UNIT_TILES[unit], 2, P], F32, tag="z_ps")
            else:
                xt_ps = psum_x.tile([P, UNIT_TILES[unit], 2, P], F32, tag="x_ps")
            for j in range(UNIT_TILES[unit]):
                words = x_tiles[unit][:, j, :].bitcast(F32)
                for u in range(2):
                    nc.tensor.transpose(xt_ps[:, j, u, :], words[:, u::2], ident[:])
            live["xt_ps", unit] = xt_ps

        def copy_x(unit):
            if unit not in units:
                return
            x_words = per_unit.tile([P, UNIT_TILES[unit], P, 2], F32, align_bytes=64)
            copy = nc.vector.tensor_copy if unit in X_BY_VECTOR else nc.scalar.copy
            copy(out=x_words[:], in_=live.pop(("xt_ps", unit))[:].rearrange("p j u r -> p j r u"))
            live["x_words", unit] = x_words

        def quantise_x(unit):
            if unit not in units:
                return
            x_words = live.pop(("x_words", unit))
            x_codes = per_unit.tile([P, UNIT_TILES[unit] * P], U32, align_bytes=64)
            x_scales = per_unit.tile([P, UNIT_TILES[unit] * P], U8, align_bytes=64)
            nc.vector.quantize_mx(
                out=x_codes[:].bitcast(FP8X4),
                scales=x_scales[:],
                in_=x_words[:].rearrange("p j r u -> p (j r u)").bitcast(BF16),
            )
            live["x_q", unit] = x_codes, x_scales

        def first_matmul(unit):
            if unit not in units:
                return
            x_codes, x_scales = live.pop(("x_q", unit))
            for j in range(UNIT_TILES[unit]):
                tokens = slice(j * P, (j + 1) * P)
                h_ps = psum_h.tile([P, H], F32, tag="h_ps")
                nc.tensor.matmul_mx(
                    out=h_ps[:],
                    lhsT=x_codes[:, tokens].bitcast(FP8X4),
                    lhsT_scale=x_scales[:, tokens],
                    rhs=w1_codes[:].bitcast(FP8X4),
                    rhs_scale=w1_scales[:],
                    start=True,
                    stop=True,
                )
                live["h_ps", unit, j] = h_ps

        def bias_and_squares(unit):
            if unit not in units:
                return
            h_sum = per_unit.tile([P, UNIT_TILES[unit]], F32)
            sq_sum = per_unit.tile([P, UNIT_TILES[unit]], F32)
            h_tiles = []
            for j in range(UNIT_TILES[unit]):
                h = per_tile.tile([P, H], F32)
                nc.vector.scalar_tensor_tensor(
                    out=h[:],
                    in0=live.pop(("h_ps", unit, j))[:],
                    scalar=1.0,
                    in1=b1_rows[:],
                    op0=ALU.mult,
                    op1=ALU.add,
                    accum_out=h_sum[:, j : j + 1],
                )
                h_tiles.append(h)
            for j in range(UNIT_TILES[unit]):
                squares = per_tile.tile([P, H], BF16)
                nc.scalar.activation(
                    out=squares[:],
                    in_=h_tiles[j][:],
                    func=ACT.Square,
                    bias=h_sum[:, j : j + 1],
                    scale=-1.0 * H,
                    accum_out=sq_sum[:, j : j + 1],
                )
            live["h", unit] = h_tiles
            live["h_sum", unit] = h_sum
            live["sq_sum", unit] = sq_sum

        def inverse_deviation(unit):
            if unit not in units:
                return
            sq_sum = live.pop(("sq_sum", unit))
            rstd = per_unit.tile([P, UNIT_TILES[unit]], F32)
            nc.scalar.activation(
                out=rstd[:], in_=sq_sum[:], func=ACT.Abs_reciprocal_sqrt, bias=eps[:], scale=1.0 / (H * H * H)
            )
            live["rstd", unit] = rstd

        def normalise(unit):
            if unit not in units:
                return
            h_tiles = live.pop(("h", unit))
            h_sum = live.pop(("h_sum", unit))
            rstd = live.pop(("rstd", unit))
            neg_mean = per_unit.tile([P, UNIT_TILES[unit]], F32)
            nc.vector.tensor_scalar(out=neg_mean[:], in0=h_sum[:], scalar1=-1.0 / H, scalar2=None, op0=ALU.mult)
            for j in range(UNIT_TILES[unit]):
                z = per_tile.tile([P, H], F32)
                nc.gpsimd.tensor_scalar(
                    out=z[:],
                    in0=h_tiles[j][:],
                    scalar1=neg_mean[:, j : j + 1],
                    scalar2=rstd[:, j : j + 1],
                    op0=ALU.add,
                    op1=ALU.mult,
                )
                live["z", unit, j] = z

        def to_features(unit):
            if unit not in units:
                return
            z_tiles = [live.pop(("z", unit, j)) for j in range(UNIT_TILES[unit])]
            r_planes = per_unit.tile([P, PACK, UNIT_TILES[unit] * P], BF16)
            z_banks = []
            for pair in range(PACK // 2):
                z_ps = psum_z.tile([P, 2, UNIT_TILES[unit] * P], F32, tag="z_ps")
                z_banks.append(z_ps)
            for j in range(UNIT_TILES[unit]):
                for t in range(PACK):
                    nc.tensor.transpose(
                        z_banks[t // 2][:, t % 2, j * P : (j + 1) * P], z_tiles[j][:, t * P : (t + 1) * P], ident[:]
                    )
            for t in range(PACK):
                nc.scalar.activation(
                    out=r_planes[:, t, :],
                    in_=z_banks[t // 2][:, t % 2, :],
                    func=ACT.Relu,
                    bias=beta_col(t),
                    scale=gamma_col(t),
                )
            live["r_planes", unit] = r_planes

        def regroup_r(unit):
            if unit not in units:
                return
            r_planes = live.pop(("r_planes", unit))
            r_grouped = live["r_grouped", unit]
            if by_vector(unit) > 0:
                tokens = slice(0, by_vector(unit) * P)
                nc.vector.tensor_copy(
                    out=r_grouped[:, tokens, :].rearrange("p (c i) t -> p c t i", i=RUN),
                    in_=r_planes[:, :, tokens].rearrange("p t (c i) -> p c t i", i=RUN),
                )

        def by_vector(unit):
            return UNIT_TILES[unit] if unit < FULL else 1

        def regroup_by_tensor(unit):
            if unit not in units:
                return
            r_grouped = per_unit.tile([P, UNIT_TILES[unit] * P, PACK], BF16, align_bytes=64)
            live["r_grouped", unit] = r_grouped
            for j in range(by_vector(unit), UNIT_TILES[unit]):
                rg_ps = psum_x.tile([P, P, PACK], BF16, tag="x_ps")
                nc.tensor.matmul(
                    out=rg_ps[:].rearrange("p r t -> p (r t)"),
                    lhsT=ident_bf[:],
                    rhs=live["r_planes", unit][:, :, j * P : (j + 1) * P].rearrange("p t r -> p r t"),
                    start=True,
                    stop=True,
                )
                live["rg_ps", unit, j] = rg_ps

        def copy_regrouped(unit):
            if unit not in units:
                return
            for j in range(by_vector(unit), UNIT_TILES[unit]):
                nc.scalar.copy(out=live["r_grouped", unit][:, j * P : (j + 1) * P, :], in_=live.pop(("rg_ps", unit, j))[:])

        def quantise_r(unit):
            if unit not in units:
                return
            r_grouped = live.pop(("r_grouped", unit))
            r_codes = per_unit.tile([P, UNIT_TILES[unit] * P], U32, align_bytes=64)
            r_scales = per_unit.tile([P, UNIT_TILES[unit] * P], U8, align_bytes=64)
            nc.vector.quantize_mx(
                out=r_codes[:].bitcast(FP8X4),
                scales=r_scales[:],
                in_=r_grouped[:].rearrange("p r t -> p (r t)"),
            )
            live["r_codes", unit] = r_codes
            live["r_scales", unit] = r_scales

        def second_matmuls(unit):
            if unit not in units:
                return
            r_codes = live.pop(("r_codes", unit))
            r_scales = live.pop(("r_scales", unit))
            w2_codes, w2_scales = w2_q["codes"], w2_q["scales"]
            x1t_ps = psum_b.tile([P, HALVES, UNIT_TILES[unit] * P], F32, tag="x1t_ps")
            for c in range(HALVES):
                channels = slice(c * P, (c + 1) * P)
                nc.tensor.matmul_mx(
                    out=x1t_ps[:, c, :],
                    lhsT=w2_codes[:, channels].bitcast(FP8X4),
                    lhsT_scale=w2_scales[:, channels],
                    rhs=r_codes[:].bitcast(FP8X4),
                    rhs_scale=r_scales[:],
                    start=True,
                    stop=True,
                )
            x1_ps = psum_a.tile([P, UNIT_TILES[unit], G], F32, tag="x1_ps")
            for j in range(UNIT_TILES[unit]):
                tokens = slice(j * P, (j + 1) * P)
                nc.tensor.matmul_mx(
                    out=x1_ps[:, j, :],
                    lhsT=r_codes[:, tokens].bitcast(FP8X4),
                    lhsT_scale=r_scales[:, tokens],
                    rhs=w2_codes[:].bitcast(FP8X4),
                    rhs_scale=w2_scales[:],
                    start=True,
                    stop=True,
                )
            live["x1_ps", unit] = x1_ps
            live["x1t_ps", unit] = x1t_ps

        def group_of(unit):
            g = max(n for n in range(len(GROUP_TILES)) if GROUP_START[n] <= UNIT_START[unit])
            return g, UNIT_START[unit] - GROUP_START[g]

        def closed_group(unit):
            if unit not in units:
                return None
            g, tile_in_group = group_of(unit)
            return g if tile_in_group + UNIT_TILES[unit] == GROUP_TILES[g] else None

        def outputs(unit):
            if unit not in units:
                return
            g, tile_in_group = group_of(unit)
            if tile_in_group == 0:
                pooled_new = per_unit.tile([P, HALVES, GROUP_TILES[g] * LINES_PER_TILE], F32)
                live["pooled", g] = pooled_new
            first_line = tile_in_group * LINES_PER_TILE
            nc.vector.tensor_reduce(
                out=live["pooled", g][:, :, first_line : first_line + UNIT_TILES[unit] * LINES_PER_TILE],
                in_=live.pop(("x1t_ps", unit))[:].rearrange("p c (b l) -> p c b l", l=NODES),
                axis=AXIS.X,
                op=ALU.max,
            )
            x1 = stores.tile([P, UNIT_TILES[unit], G], F32)
            nc.vector.tensor_tensor(
                out=x1[:],
                in0=live.pop(("x1_ps", unit))[:],
                in1=b2_rows[:].unsqueeze(1).to_broadcast([P, UNIT_TILES[unit], G]),
                op=ALU.add,
            )
            nc.sync.dma_start(
                out=out_flat[rows_of(unit), 0:G].rearrange("(j p) c -> p j c", p=P),
                in_=x1[:],
            )

        def spread_maxima(unit):
            g = closed_group(unit)
            if g is None:
                return
            lines = GROUP_TILES[g] * LINES_PER_TILE
            copies = P // lines
            pooled = live.pop(("pooled", g))
            spread = per_unit.tile([P, HALVES, lines, copies], F32)
            for c in range(HALVES):
                nc.scalar.activation(
                    out=spread[:, c, :, :],
                    in_=pooled[:, c, :].unsqueeze(2).to_broadcast([P, lines, copies]),
                    func=ACT.Identity,
                    bias=b2_col(c),
                )
            live["spread", g] = spread

        def pool(unit):
            g = closed_group(unit)
            if g is None:
                return
            lines = GROUP_TILES[g] * LINES_PER_TILE
            copies = P // lines
            spread = live.pop(("spread", g))
            x2_ps = psum_x.tile([P, G], F32, tag="x_ps")
            for c in range(HALVES):
                nc.tensor.transpose(
                    x2_ps[:, c * P : (c + 1) * P],
                    spread[:, c, :, :].rearrange("p b d -> p (b d)"),
                    ident[:],
                )
            x2 = per_unit.tile([P, G], F32)
            nc.scalar.copy(out=x2[:], in_=x2_ps[:])
            nc.sync.dma_start(
                out=out_flat[GROUP_START[g] * P : (GROUP_START[g] + GROUP_TILES[g]) * P, G : 2 * G].rearrange(
                    "(q i) c -> q i c", i=NODES // copies
                ),
                in_=x2[:].unsqueeze(1).to_broadcast([P, NODES // copies, G]),
            )

        for k in range(N_UNITS + S_POOL):
            spread_maxima(k - S_POOL)
            bias_and_squares(k - S_NORM)
            outputs(k - S_OUTPUTS)
            draining = k - S_NORM >= N_UNITS
            if draining:
                to_features(k - S_FEATURES)
                pool(k - S_POOL)
                second_matmuls(k - S_SECOND)
            copy_x(k - S_COPY_X)
            inverse_deviation(k - S_NORM)
            if not draining:
                to_features(k - S_FEATURES)
            regroup_by_tensor(k - S_REGROUP)
            copy_regrouped(k - S_REGROUP)
            regroup_r(k - S_REGROUP)
            first_matmul(k - S_FIRST)
            if not draining:
                second_matmuls(k - S_SECOND)
            quantise_x(k - S_QUANTISE_X)
            if not draining:
                pool(k - S_POOL)
            quantise_r(k - S_QUANTISE_R)
            normalise(k - S_NORM)
            if k == S_QUANTISE_X:
                regroup_w2()
            if k == S_FIRST:
                spread_b2()
            if k == S_COPY_X:
                spread_b1()
            transpose_x(k - S_TRANSPOSE_X)
            if k == S_NORM:
                nc.vector.tensor_copy(out=affine[:], in_=affine_bf[:, :, 0:PACK])
                w2_q["codes"], w2_q["scales"] = quantise_weight(w2_grouped, G, "w2")
